import numpy as np
import ml_dtypes


def mxq(x, axis, fmt="e4m3"):
    dtype, down = {"e4m3": (ml_dtypes.float8_e4m3fn, 7), "e5m2": (ml_dtypes.float8_e5m2, 14)}[fmt]
    v = np.moveaxis(np.asarray(x, np.float32).astype(ml_dtypes.bfloat16).astype(np.float64), axis, -1)
    blocks = v.reshape(v.shape[:-1] + (-1, 32))
    amax = np.abs(blocks).max(-1, keepdims=True)
    byte = np.maximum(np.where(amax > 0, np.frexp(amax)[1] - 1 + 127, 0) - down, 1)
    scale = np.exp2(byte - 127.0)
    codes = (blocks / scale).astype(np.float32).astype(dtype).astype(np.float64)
    return np.moveaxis((codes * scale).reshape(v.shape), -1, axis)


WIDE = False


def mx_kscale(k):
    if not WIDE:
        return np.ones(k)
    levels = np.array([18, -18])
    if k % 512:
        return np.exp2(np.random.permutation(np.resize(levels, k // 32))).repeat(32)
    a = np.empty((k // 512, 16))
    for p in range(k // 512):
        a[p, :8] = np.random.permutation(np.resize(levels, 8))
        for g in range(8):
            far = levels[np.abs(levels - a[p, g]) >= 10]
            a[p, g + 8] = far[np.random.randint(len(far))]
    return np.exp2(a.ravel()).repeat(32)


BF16 = ml_dtypes.bfloat16


def bf(x):
    return np.asarray(x, np.float32).astype(BF16)


def f64(x):
    return np.asarray(x).astype(np.float64)


B, HH, WW, C, NH, KD, WS, SS = 1, 32, 64, 512, 8, 64, 8, 4
GH, GW, T, F = HH // WS, WW // WS, WS * WS, NH * KD
N = B * GH * GW


def to_windows(a):
    c = a.shape[-1]
    r = np.roll(a, shift=(-SS, -SS), axis=(1, 2))
    return r.reshape(B, GH, WS, GW, WS, c).swapaxes(2, 3).reshape(N * T, c)


def from_windows(a):
    c = a.shape[-1]
    r = a.reshape(B, GH, GW, WS, WS, c).swapaxes(2, 3).reshape(B, HH, WW, c)
    return np.roll(r, shift=(SS, SS), axis=(1, 2))


def setup_inputs():
    s = mx_kscale(N * T)
    sx = from_windows(s[:, None])
    sg = s.reshape(N, T, 1, 1)
    uq = mx_kscale(F).reshape(NH, KD)
    uk = mx_kscale(F).reshape(NH, KD)
    uv = mx_kscale(F).reshape(NH, KD)

    def weight(u):
        return bf(np.random.standard_normal((C, NH, KD)) / np.sqrt(C) / u)

    def bias():
        return bf(np.random.standard_normal((NH, KD)) * 0.3)

    def grad(u):
        e = np.exp2(np.random.randint(-6, 1, (N, T, 1, 1)))
        return bf(np.random.standard_normal((N, T, NH, KD)) * e / sg * u)

    return {"x": bf(np.random.standard_normal((B, HH, WW, C)) * sx), "wq": weight(uq), "bq": bias(),
            "wk": weight(uk), "bk": bias(), "wv": weight(uv), "bv": bias(),
            "grad_0": grad(uq), "grad_1": grad(uk), "grad_2": grad(uv)}


def reference(x, wq, bq, wk, bk, wv, bv, grad_0, grad_1, grad_2):
    win = to_windows(f64(x))
    g = np.concatenate([f64(grad_0).reshape(N * T, F), f64(grad_1).reshape(N * T, F),
                        f64(grad_2).reshape(N * T, F)], axis=1)
    w = np.concatenate([f64(wq).reshape(C, F), f64(wk).reshape(C, F), f64(wv).reshape(C, F)], axis=1)
    dwin = mxq(g, 1, "e5m2") @ mxq(w, 1, "e4m3").T
    dw = mxq(win, 0, "e4m3").T @ mxq(g, 0, "e5m2")
    dx = from_windows(dwin)
    dwq = dw[:, :F].reshape(C, NH, KD)
    dwk = dw[:, F:2 * F].reshape(C, NH, KD)
    dwv = dw[:, 2 * F:].reshape(C, NH, KD)
    return dx, dwq, dwk, dwv

@@ -1,0 +1,249 @@
+from contextlib import ExitStack
+
+import concourse.mybir as mybir
+from concourse.masks import make_identity
+
+F32 = mybir.dt.float32
+BF16 = mybir.dt.bfloat16
+U32 = mybir.dt.uint32
+U8 = mybir.dt.uint8
+E4M3 = mybir.dt.float8_e4m3fn_x4
+E5M2 = mybir.dt.float8_e5m2_x4
+
+P = 128
+PACK = 4
+C = 512
+F = 512
+LAYERS = 3
+PASSES = 4
+WIN = 8
+SHIFT = 4
+ROWS = 32
+QUADS = 16
+HALVES = 2 * PASSES
+C_TILES = C // P
+
+FLOPS = 2 * 2 * 2048 * 512 * 1536
+BYTES = 2 * (2048 * 512 + 3 * 512 * 512 + 3 * 2048 * 512) + 4 * (2048 * 512 + 3 * 512 * 512)
+
+
+def tile_windowattentionblock_pa_v_kernel(
+    tc, x, wq, bq, wk, bk, wv, bv, grad_0, grad_1, grad_2, out_0, out_1, out_2, out_3
+):
+    nc = tc.nc
+    weights = [w.rearrange("(j p) h d -> p j (h d)", p=P) for w in (wq, wk, wv)]
+    grads = [
+        g.rearrange("n t h d -> (n t) (h d)").rearrange("(r p j) f -> r p j f", p=P, j=PACK)
+        for g in (grad_0, grad_1, grad_2)
+    ]
+    x_quads = x.rearrange("b r (q j) c -> (b r) q (j c)", j=PACK)
+    dx_quads = out_0.rearrange("b r (q j) c -> (b r q) j c", j=PACK)
+    dws = [o.rearrange("(t p) h d -> t p (h d)", p=P) for o in (out_1, out_2, out_3)]
+
+    with ExitStack() as ctx:
+        keep = ctx.enter_context(tc.tile_pool(name="keep", bufs=1))
+        stage = ctx.enter_context(tc.tile_pool(name="stage", bufs=4))
+        turned_codes = ctx.enter_context(tc.tile_pool(name="turned_codes", bufs=9))
+        results = ctx.enter_context(tc.tile_pool(name="results", bufs=8))
+        psum_turn = ctx.enter_context(tc.psum_pool(name="psum_turn", bufs=4))
+        psum_sum = ctx.enter_context(tc.psum_pool(name="psum_sum", bufs=4))
+        ctx.enter_context(tc.manual_schedule())
+
+        w_raw = [keep.tile([P, PACK, F], BF16, name="w_raw%d" % s) for s in range(LAYERS)]
+        g_raw = [
+            [keep.tile([P, PACK, F], BF16, name="g_raw%d_%d" % (s, r)) for r in range(PASSES)] for s in range(LAYERS)
+        ]
+        x_head = keep.tile([P, PASSES - 1, PACK * C], BF16, name="x_head")
+        x_last = keep.tile([P, PACK * C], BF16, name="x_last")
+
+        def load_g(s, r):
+            nc.sync.dma_start(out=g_raw[s][r][:], in_=grads[s][r])
+
+        def load_x_head(gj, h):
+            quad = (2 * gj + h + 1) % QUADS
+            rows = x_quads[SHIFT : SHIFT + (PASSES - 1) * WIN, quad, :]
+            nc.sync.dma_start(
+                out=x_head[2 * WIN * gj + h : 2 * WIN * (gj + 1) : 2, :, :],
+                in_=rows.rearrange("(r t) e -> t r e", t=WIN),
+            )
+
+        def load_x_last():
+            for ti in range(WIN):
+                row = ((PASSES - 1) * WIN + ti + SHIFT) % ROWS
+                nc.sync.dma_start(out=x_last[2 * ti : P : 2 * WIN, :], in_=x_quads[row, 1:QUADS:2, :])
+                nc.sync.dma_start(out=x_last[2 * ti + 1 : P - 2 * WIN : 2 * WIN, :], in_=x_quads[row, 2:QUADS:2, :])
+            for half in range(2):
+                first = P - 2 * WIN + WIN * half + 1
+                row = ((PASSES - 1) * WIN + SHIFT * half + SHIFT) % ROWS
+                nc.sync.dma_start(out=x_last[first : first + WIN - 1 : 2, :], in_=x_quads[row : row + SHIFT, 0, :])
+
+        for s in range(LAYERS):
+            nc.sync.dma_start(out=w_raw[s][:], in_=weights[s])
+            load_g(s, 0)
+        for s in range(LAYERS):
+            load_g(s, 1)
+        x_parts = [(gj, h) for gj in range(WIN) for h in range(2)]
+        for i in range(2 * LAYERS):
+            load_g(i % LAYERS, 2 + i // LAYERS)
+            for gj, h in x_parts[3 * i : 3 * i + 3]:
+                load_x_head(gj, h)
+        load_x_last()
+
+        identity = keep.tile([P, P], F32, name="identity")
+        make_identity(nc, identity[:])
+        to_image = keep.tile([P, P], F32, name="to_image")
+        src = identity[:].rearrange("p (gj ti h) -> p ti gj h", ti=WIN, h=2)
+        dst = to_image[:].rearrange("p (ti a e) -> p ti a e", ti=WIN, e=2)
+        nc.vector.tensor_copy(out=dst[:, :, :, 1], in_=src[:, :, :, 0])
+        nc.vector.tensor_copy(out=dst[:, :, 1:WIN, 0], in_=src[:, :, 0 : WIN - 1, 1])
+        nc.vector.tensor_copy(out=dst[:, :, 0:1, 0], in_=src[:, :, WIN - 1 : WIN, 1])
+
+        def turn(raw, pair, moving, grouped):
+            words = raw[:].bitcast(F32)
+            bank = psum_turn.tile([P, 2, 2, P], F32, name="bank")
+            for j in range(2):
+                for u in range(2):
+                    nc.tensor.transpose(bank[:, j, u, :], words[:, 2 * pair + j, u : F // 2 : 2], moving[:])
+            nc.scalar.copy(
+                out=grouped.bitcast(F32).rearrange("p (j r u) -> p j r u", j=2, u=2),
+                in_=bank[:].rearrange("p j u r -> p j r u"),
+            )
+
+        def quantize(grouped, codes, scales, fmt):
+            nc.vector.quantize_mx(out=codes.bitcast(fmt), scales=scales, in_=grouped)
+
+        w_mx = []
+        token_mx = {}
+
+        def token_source(key):
+            s, r = key
+            if s < LAYERS:
+                return g_raw[s][r][:]
+            flat = x_head[:, r, :] if r < PASSES - 1 else x_last[:]
+            return flat.rearrange("p (j c) -> p j c", j=PACK)
+
+        def interleave(key):
+            grouped = stage.tile([P, F * PACK], BF16, name="token_grouped", align_bytes=64)
+            nc.vector.tensor_copy(
+                out=grouped[:].rearrange("p (c i t) -> p c t i", i=4, t=PACK),
+                in_=token_source(key).rearrange("p t (c i) -> p c t i", i=4),
+            )
+            return grouped
+
+        def quantize_tokens(key, grouped):
+            codes = keep.tile([P, F], U32, name="token_codes%d_%d" % key, align_bytes=64)
+            scales = keep.tile([P, F], U8, name="token_scales%d_%d" % key, align_bytes=64)
+            quantize(grouped[:], codes[:], scales[:], E5M2 if key[0] < LAYERS else E4M3)
+            token_mx[key] = (codes, scales)
+
+        def turn_weight(s):
+            grouped = stage.tile([P, C * PACK], BF16, name="w_grouped", align_bytes=64, bufs=2)
+            for pair in range(2):
+                turn(w_raw[s], pair, identity, grouped[:, pair * 2 * P * PACK : (pair + 1) * 2 * P * PACK])
+            codes = keep.tile([P, C], U32, name="w_codes%d" % s, align_bytes=64)
+            scales = keep.tile([P, C], U8, name="w_scales%d" % s, align_bytes=64)
+            quantize(grouped[:], codes[:], scales[:], E4M3)
+            w_mx.append((codes, scales))
+
+        def turn_grad(s, half):
+            grouped = stage.tile([P, 2 * P * PACK], BF16, name="g_grouped", align_bytes=64)
+            turn(g_raw[s][half // 2], half % 2, to_image, grouped[:])
+            return grouped
+
+        def quantize_grad(grouped):
+            codes = turned_codes.tile([P, 2 * P], U32, name="g_codes", align_bytes=64)
+            scales = turned_codes.tile([P, 2 * P], U8, name="g_scales", align_bytes=64)
+            quantize(grouped[:], codes[:], scales[:], E5M2)
+            return codes, scales
+
+        def mx(acc, stationary, cols, stationary_fmt, moving, moving_fmt, first, last):
+            nc.tensor.matmul_mx(
+                out=acc[:],
+                lhsT=stationary[0][:, cols].bitcast(stationary_fmt),
+                lhsT_scale=stationary[1][:, cols],
+                rhs=moving[0][:].bitcast(moving_fmt),
+                rhs_scale=moving[1][:],
+                start=first,
+                stop=last,
+            )
+
+        def dx_pass(accs, turned, s, j):
+            mx(accs[j], turned[s], slice(j * P, (j + 1) * P), E5M2, w_mx[s], E4M3, s == 0, s == LAYERS - 1)
+
+        def new_accs():
+            return [psum_sum.tile([P, C], F32, name="acc") for j in range(2)]
+
+        def store_dx(accs, half):
+            r, pair = divmod(half, 2)
+            result = results.tile([P, 2, C], F32, name="dx_result")
+            for j in range(2):
+                nc.scalar.copy(out=result[:, j, :], in_=accs[j][:])
+            first = (r * WIN + SHIFT) * QUADS
+            slots = slice(2 * pair, 2 * pair + 2)
+            if r < PASSES - 1:
+                nc.sync.dma_start(out=dx_quads[first : first + P, slots, :], in_=result[:])
+            else:
+                nc.sync.dma_start(out=dx_quads[first : first + P // 2, slots, :], in_=result[0 : P // 2])
+                nc.sync.dma_start(out=dx_quads[0 : P // 2, slots, :], in_=result[P // 2 : P])
+
+        X = LAYERS
+        token_work = [
+            [(0, 0), (1, 0)], [(2, 0)], [(0, 1), (1, 1)], [(2, 1)],
+            [(0, 2), (1, 2)], [(X, 0)], [(X, 1), (X, 2)], [(0, 3)],
+        ]
+        late_work = [(X, 3), (1, 3), (2, 2), (2, 3)]
+
+        turned = []
+        accs = new_accs()
+        for s in range(LAYERS):
+            turn_weight(s)
+            grouped = turn_grad(s, 0)
+            if s < 2:
+                key = token_work[0][s]
+                tokens = interleave(key)
+            turned.append(quantize_grad(grouped))
+            if s < 2:
+                quantize_tokens(key, tokens)
+            if s > 0:
+                for j in range(2):
+                    dx_pass(accs, turned, s - 1, j)
+
+        for half in range(1, HALVES + 1):
+            before = turned
+            if half < HALVES:
+                keys = token_work[half]
+                turned = []
+                tokens = interleave(keys[0])
+                turned.append(quantize_grad(turn_grad(0, half)))
+                quantize_tokens(keys[0], tokens)
+                turned.append(quantize_grad(turn_grad(1, half)))
+                if len(keys) > 1:
+                    tokens = interleave(keys[1])
+                turned.append(quantize_grad(turn_grad(2, half)))
+                if len(keys) > 1:
+                    quantize_tokens(keys[1], tokens)
+            if half == 1:
+                for j in range(2):
+                    dx_pass(accs, before, LAYERS - 1, j)
+            else:
+                accs = new_accs()
+                for j in range(2):
+                    for s in range(LAYERS):
+                        dx_pass(accs, before, s, j)
+            store_dx(accs, half - 1)
+
+        tokens = [interleave(late_work[0])]
+        for i in range(len(late_work)):
+            if i + 1 < len(late_work):
+                tokens.append(interleave(late_work[i + 1]))
+            quantize_tokens(late_work[i], tokens[i])
+
+        for s in range(LAYERS):
+            for t in range(C_TILES):
+                acc = psum_sum.tile([P, F], F32, name="acc")
+                for r in range(PASSES):
+                    mx(acc, token_mx[(X, r)], slice(t * P, (t + 1) * P), E4M3, token_mx[(s, r)], E5M2,
+                       r == 0, r == PASSES - 1)
+                result = results.tile([P, F], F32, name="dw_result", bufs=4)
+                nc.scalar.copy(out=result[:], in_=acc[:])
+                nc.sync.dma_start(out=dws[s][t], in_=result[:])

@@ -12,16 +12,16 @@ E5M2 = mybir.dt.float8_e5m2_x4
 
 P = 128
 PACK = 4
-C = 512
-F = 512
+WIDTH = 512
 LAYERS = 3
 PASSES = 4
 WIN = 8
 SHIFT = 4
 ROWS = 32
 QUADS = 16
-HALVES = 2 * PASSES
-C_TILES = C // P
+X = LAYERS
+DIRECT = 2
+HELD_BACK = 2
 
 FLOPS = 2 * 2 * 2048 * 512 * 1536
 BYTES = 2 * (2048 * 512 + 3 * 512 * 512 + 3 * 2048 * 512) + 4 * (2048 * 512 + 3 * 512 * 512)
@@ -33,217 +33,302 @@ def tile_windowattentionblock_pa_v_kernel(
     nc = tc.nc
     weights = [w.rearrange("(j p) h d -> p j (h d)", p=P) for w in (wq, wk, wv)]
     grads = [
-        g.rearrange("n t h d -> (n t) (h d)").rearrange("(r p j) f -> r p j f", p=P, j=PACK)
+        g.rearrange("n t h d -> (n t) (h d)").rearrange("(r p j) f -> r p (j f)", p=P, j=PACK)
         for g in (grad_0, grad_1, grad_2)
     ]
-    x_quads = x.rearrange("b r (q j) c -> (b r) q (j c)", j=PACK)
-    dx_quads = out_0.rearrange("b r (q j) c -> (b r q) j c", j=PACK)
-    dws = [o.rearrange("(t p) h d -> t p (h d)", p=P) for o in (out_1, out_2, out_3)]
+    x_quads = x.rearrange("b row (q j) c -> (b row) q (j c)", j=PACK)
+    x_image = x_quads.rearrange("row q e -> (row q) e")
+    dx_image = out_0.rearrange("b row (q j) c -> (b row q) j c", j=PACK)
+    dws = [o.rearrange("(m p) h d -> m p (h d)", p=P) for o in (out_1, out_2, out_3)]
 
     with ExitStack() as ctx:
         keep = ctx.enter_context(tc.tile_pool(name="keep", bufs=1))
         stage = ctx.enter_context(tc.tile_pool(name="stage", bufs=4))
-        turned_codes = ctx.enter_context(tc.tile_pool(name="turned_codes", bufs=9))
         results = ctx.enter_context(tc.tile_pool(name="results", bufs=8))
         psum_turn = ctx.enter_context(tc.psum_pool(name="psum_turn", bufs=4))
         psum_sum = ctx.enter_context(tc.psum_pool(name="psum_sum", bufs=4))
         ctx.enter_context(tc.manual_schedule())
 
-        w_raw = [keep.tile([P, PACK, F], BF16, name="w_raw%d" % s) for s in range(LAYERS)]
+        w_raw = [[keep.tile([P, 2 * WIDTH], BF16, name="w_raw%d_%d" % (s, a)) for a in range(2)] for s in range(LAYERS)]
         g_raw = [
-            [keep.tile([P, PACK, F], BF16, name="g_raw%d_%d" % (s, r)) for r in range(PASSES)] for s in range(LAYERS)
+            [keep.tile([P, PACK * WIDTH], BF16, name="g_raw%d_%d" % (s, r)) for r in range(PASSES)]
+            for s in range(LAYERS)
         ]
-        x_head = keep.tile([P, PASSES - 1, PACK * C], BF16, name="x_head")
-        x_last = keep.tile([P, PACK * C], BF16, name="x_last")
+        x_direct = keep.tile([P, DIRECT, PACK * WIDTH], BF16, name="x_direct")
+        x_raw = {r: keep.tile([P, PACK * WIDTH], BF16, name="x_raw%d" % r) for r in range(DIRECT, PASSES)}
 
-        def load_g(s, r):
-            nc.sync.dma_start(out=g_raw[s][r][:], in_=grads[s][r])
+        def image_ranges(r):
+            first = (r * WIN + SHIFT) * QUADS
+            if r < PASSES - 1:
+                return [(slice(0, P), slice(first, first + P))]
+            return [(slice(0, P // 2), slice(first, first + P // 2)), (slice(P // 2, P), slice(0, P // 2))]
 
-        def load_x_head(gj, h):
-            quad = (2 * gj + h + 1) % QUADS
-            rows = x_quads[SHIFT : SHIFT + (PASSES - 1) * WIN, quad, :]
-            nc.sync.dma_start(
-                out=x_head[2 * WIN * gj + h : 2 * WIN * (gj + 1) : 2, :, :],
-                in_=rows.rearrange("(r t) e -> t r e", t=WIN),
-            )
+        def load_g(r, cols):
+            for s in range(LAYERS):
+                nc.sync.dma_start(out=g_raw[s][r][:, cols], in_=grads[s][r][:, cols])
 
-        def load_x_last():
-            for ti in range(WIN):
-                row = ((PASSES - 1) * WIN + ti + SHIFT) % ROWS
-                nc.sync.dma_start(out=x_last[2 * ti : P : 2 * WIN, :], in_=x_quads[row, 1:QUADS:2, :])
-                nc.sync.dma_start(out=x_last[2 * ti + 1 : P - 2 * WIN : 2 * WIN, :], in_=x_quads[row, 2:QUADS:2, :])
+        def load_x_image(r):
+            for parts, quads in image_ranges(r):
+                nc.sync.dma_start(out=x_raw[r][parts, :], in_=x_image[quads, :])
+
+        first_half, second_half = slice(0, 2 * WIDTH), slice(2 * WIDTH, PACK * WIDTH)
+        for s in range(LAYERS):
             for half in range(2):
-                first = P - 2 * WIN + WIN * half + 1
-                row = ((PASSES - 1) * WIN + SHIFT * half + SHIFT) % ROWS
-                nc.sync.dma_start(out=x_last[first : first + WIN - 1 : 2, :], in_=x_quads[row : row + SHIFT, 0, :])
+                nc.sync.dma_start(
+                    out=w_raw[s][half][:].rearrange("p (j f) -> p j f", j=2),
+                    in_=weights[s][:, 2 * half : 2 * half + 2, :],
+                )
+            nc.sync.dma_start(out=g_raw[s][0][:, first_half], in_=grads[s][0][:, first_half])
+        load_g(0, second_half)
+        for r in range(1, PASSES):
+            load_g(r, slice(0, PACK * WIDTH))
+            if r <= PASSES - DIRECT:
+                load_x_image(PASSES - r)
+        for h in range(2):
+            for n in range(WIN):
+                gj = n // 2 + (n % 2) * (WIN // 2)
+                rows = x_quads[SHIFT : SHIFT + DIRECT * WIN, (2 * gj + h + 1) % QUADS, :]
+                nc.sync.dma_start(
+                    out=x_direct[2 * WIN * gj + h : 2 * WIN * (gj + 1) : 2, :, :],
+                    in_=rows.rearrange("(r ti) e -> ti r e", ti=WIN),
+                )
 
-        for s in range(LAYERS):
-            nc.sync.dma_start(out=w_raw[s][:], in_=weights[s])
-            load_g(s, 0)
-        for s in range(LAYERS):
-            load_g(s, 1)
-        x_parts = [(gj, h) for gj in range(WIN) for h in range(2)]
-        for i in range(2 * LAYERS):
-            load_g(i % LAYERS, 2 + i // LAYERS)
-            for gj, h in x_parts[3 * i : 3 * i + 3]:
-                load_x_head(gj, h)
-        load_x_last()
+        def quad_copies(window_cols, image_cols):
+            win = window_cols.rearrange("p (gj ti h) -> p ti gj h", ti=WIN, h=2)
+            img = image_cols.rearrange("p (ti a e) -> p ti a e", ti=WIN, e=2)
+            return [
+                (win[:, :, :, 0], img[:, :, :, 1]),
+                (win[:, :, 0 : WIN - 1, 1], img[:, :, 1:WIN, 0]),
+                (win[:, :, WIN - 1 : WIN, 1], img[:, :, 0:1, 0]),
+            ]
 
         identity = keep.tile([P, P], F32, name="identity")
-        make_identity(nc, identity[:])
         to_image = keep.tile([P, P], F32, name="to_image")
-        src = identity[:].rearrange("p (gj ti h) -> p ti gj h", ti=WIN, h=2)
-        dst = to_image[:].rearrange("p (ti a e) -> p ti a e", ti=WIN, e=2)
-        nc.vector.tensor_copy(out=dst[:, :, :, 1], in_=src[:, :, :, 0])
-        nc.vector.tensor_copy(out=dst[:, :, 1:WIN, 0], in_=src[:, :, 0 : WIN - 1, 1])
-        nc.vector.tensor_copy(out=dst[:, :, 0:1, 0], in_=src[:, :, WIN - 1 : WIN, 1])
+        to_window = keep.tile([P, P], F32, name="to_window")
+        make_identity(nc, identity[:])
+        for win, img in quad_copies(identity[:], to_image[:]):
+            nc.vector.tensor_copy(out=img, in_=win)
+        for win, img in quad_copies(to_window[:], identity[:]):
+            nc.vector.tensor_copy(out=win, in_=img)
 
-        def turn(raw, pair, moving, grouped):
-            words = raw[:].bitcast(F32)
-            bank = psum_turn.tile([P, 2, 2, P], F32, name="bank")
-            for j in range(2):
-                for u in range(2):
-                    nc.tensor.transpose(bank[:, j, u, :], words[:, 2 * pair + j, u : F // 2 : 2], moving[:])
-            nc.scalar.copy(
-                out=grouped.bitcast(F32).rearrange("p (j r u) -> p j r u", j=2, u=2),
-                in_=bank[:].rearrange("p j u r -> p j r u"),
-            )
-
-        def quantize(grouped, codes, scales, fmt):
-            nc.vector.quantize_mx(out=codes.bitcast(fmt), scales=scales, in_=grouped)
-
-        w_mx = []
-        token_mx = {}
-
-        def token_source(key):
-            s, r = key
-            if s < LAYERS:
-                return g_raw[s][r][:]
-            flat = x_head[:, r, :] if r < PASSES - 1 else x_last[:]
-            return flat.rearrange("p (j c) -> p j c", j=PACK)
-
-        def interleave(key):
-            grouped = stage.tile([P, F * PACK], BF16, name="token_grouped", align_bytes=64)
-            nc.vector.tensor_copy(
-                out=grouped[:].rearrange("p (c i t) -> p c t i", i=4, t=PACK),
-                in_=token_source(key).rearrange("p t (c i) -> p c t i", i=4),
-            )
-            return grouped
-
-        def quantize_tokens(key, grouped):
-            codes = keep.tile([P, F], U32, name="token_codes%d_%d" % key, align_bytes=64)
-            scales = keep.tile([P, F], U8, name="token_scales%d_%d" % key, align_bytes=64)
-            quantize(grouped[:], codes[:], scales[:], E5M2 if key[0] < LAYERS else E4M3)
-            token_mx[key] = (codes, scales)
-
-        def turn_weight(s):
-            grouped = stage.tile([P, C * PACK], BF16, name="w_grouped", align_bytes=64, bufs=2)
-            for pair in range(2):
-                turn(w_raw[s], pair, identity, grouped[:, pair * 2 * P * PACK : (pair + 1) * 2 * P * PACK])
-            codes = keep.tile([P, C], U32, name="w_codes%d" % s, align_bytes=64)
-            scales = keep.tile([P, C], U8, name="w_scales%d" % s, align_bytes=64)
-            quantize(grouped[:], codes[:], scales[:], E4M3)
-            w_mx.append((codes, scales))
-
-        def turn_grad(s, half):
-            grouped = stage.tile([P, 2 * P * PACK], BF16, name="g_grouped", align_bytes=64)
-            turn(g_raw[s][half // 2], half % 2, to_image, grouped[:])
-            return grouped
-
-        def quantize_grad(grouped):
-            codes = turned_codes.tile([P, 2 * P], U32, name="g_codes", align_bytes=64)
-            scales = turned_codes.tile([P, 2 * P], U8, name="g_scales", align_bytes=64)
-            quantize(grouped[:], codes[:], scales[:], E5M2)
+        def quantize(pool, name, grouped, fmt, bufs=None):
+            cols = grouped.shape[1] // PACK
+            codes = pool.tile([P, cols], U32, name=name + "_codes", align_bytes=64, bufs=bufs)
+            scales = pool.tile([P, cols], U8, name=name + "_scales", align_bytes=64, bufs=bufs)
+            nc.vector.quantize_mx(out=codes[:].bitcast(fmt), scales=scales[:], in_=grouped)
             return codes, scales
 
-        def mx(acc, stationary, cols, stationary_fmt, moving, moving_fmt, first, last):
+        def multiply(acc, stationary, m_tile, stationary_fmt, moving, moving_fmt, start, stop):
+            cols = slice(m_tile * P, (m_tile + 1) * P)
             nc.tensor.matmul_mx(
                 out=acc[:],
                 lhsT=stationary[0][:, cols].bitcast(stationary_fmt),
                 lhsT_scale=stationary[1][:, cols],
                 rhs=moving[0][:].bitcast(moving_fmt),
                 rhs_scale=moving[1][:],
-                start=first,
-                stop=last,
+                start=start,
+                stop=stop,
             )
 
-        def dx_pass(accs, turned, s, j):
-            mx(accs[j], turned[s], slice(j * P, (j + 1) * P), E5M2, w_mx[s], E4M3, s == 0, s == LAYERS - 1)
+        def every_second_word(raw, half):
+            words = raw[:].bitcast(F32)
+            starts = [(2 * half + j) * 2 * P for j in range(2)]
+            return [words[:, start + u : start + 2 * P : 2] for start in starts for u in range(2)]
 
-        def new_accs():
-            return [psum_sum.tile([P, C], F32, name="acc") for j in range(2)]
+        def sorted_words(raw, half):
+            ordered = stage.tile([P, WIDTH], F32, name="ordered")
+            nc.vector.tensor_copy(
+                out=ordered[:].rearrange("p (j u q) -> p j u q", j=2, u=2),
+                in_=raw[:].bitcast(F32)[:, half * WIDTH : (half + 1) * WIDTH].rearrange(
+                    "p (j q u) -> p j u q", j=2, u=2
+                ),
+            )
+            return [ordered[:, i * P : (i + 1) * P] for i in range(4)]
 
-        def store_dx(accs, half):
-            r, pair = divmod(half, 2)
-            result = results.tile([P, 2, C], F32, name="dx_result")
+        def transpose_bank(operands, moving):
+            bank = psum_turn.tile([P, WIDTH], F32, name="bank")
+            for i, operand in enumerate(operands):
+                nc.tensor.transpose(bank[:, i * P : (i + 1) * P], operand, moving[:])
+            return bank
+
+        def turn(operands, moving, grouped):
+            bank = transpose_bank(operands, moving)
+            nc.scalar.copy(
+                out=grouped.bitcast(F32).rearrange("p (j col u) -> p j col u", j=2, u=2),
+                in_=bank[:].rearrange("p (j u col) -> p j col u", j=2, u=2),
+            )
+
+        def turn_g(operands):
+            grouped = stage.tile([P, 2 * WIDTH], BF16, name="g_turned", align_bytes=64, bufs=5)
+            turn(operands, to_image, grouped[:])
+            return grouped
+
+        def transpose_words(words, moving, name):
+            moved = stage.tile([P, 2 * WIDTH], F32, name=name, align_bytes=64, bufs=1)
+            for half in range(2):
+                blocks = [words[:, (4 * half + i) * P : (4 * half + i + 1) * P] for i in range(4)]
+                bank = transpose_bank(blocks, moving)
+                nc.scalar.copy(out=moved[:, half * WIDTH : (half + 1) * WIDTH], in_=bank[:])
+            return moved
+
+        def interleave(copy, key, grouped, cols):
+            s, r = key
+            if s < LAYERS:
+                raw = g_raw[s][r][:]
+            else:
+                raw = x_direct[:, r, :] if r < DIRECT else x_raw[r][:]
+            copy(
+                out=grouped[:, PACK * cols.start : PACK * cols.stop].rearrange("p (c i t) -> p c t i", i=4, t=PACK),
+                in_=raw.rearrange("p (t c) -> p t c", t=PACK)[:, :, cols].rearrange("p t (c i) -> p c t i", i=4),
+            )
+
+        def interleave_on_vector(key):
+            grouped = stage.tile([P, PACK * WIDTH], BF16, name="tokens", align_bytes=64, bufs=3)
+            interleave(nc.vector.tensor_copy, key, grouped, slice(0, WIDTH))
+            return grouped
+
+        def interleave_on_scalar(key, grouped, quarter):
+            interleave(nc.scalar.copy, key, grouped, slice(quarter * P, (quarter + 1) * P))
+
+        w_mx = []
+        g_mx = []
+        token_mx = {}
+        dx_sums = []
+
+        def quantize_g(grouped):
+            g_mx.append(quantize(stage, "g", grouped[:], E5M2, bufs=8))
+
+        def quantize_tokens(key, grouped):
+            token_mx[key] = quantize(keep, "tokens%d_%d" % key, grouped, E4M3 if key[0] == X else E5M2)
+
+        def multiply_dx(bank):
+            place, s = divmod(bank, LAYERS)
+            if s == 0:
+                dx_sums.append([psum_sum.tile([P, WIDTH], F32, name="acc") for j in range(2)])
             for j in range(2):
-                nc.scalar.copy(out=result[:, j, :], in_=accs[j][:])
-            first = (r * WIN + SHIFT) * QUADS
-            slots = slice(2 * pair, 2 * pair + 2)
-            if r < PASSES - 1:
-                nc.sync.dma_start(out=dx_quads[first : first + P, slots, :], in_=result[:])
+                multiply(dx_sums[place][j], g_mx[bank], j, E5M2, w_mx[s], E4M3, s == 0, s == LAYERS - 1)
+            if s == LAYERS - 1:
+                r, half = divmod(place, 2)
+                result = results.tile([P, 2, WIDTH], F32, name="result")
+                for j in range(2):
+                    nc.scalar.copy(out=result[:, j, :], in_=dx_sums[place][j][:])
+                for parts, quads in image_ranges(r):
+                    nc.sync.dma_start(out=dx_image[quads, 2 * half : 2 * half + 2, :], in_=result[parts])
+
+        w_turned = [keep.tile([P, PACK * WIDTH], BF16, name="w_turned%d" % s, align_bytes=64) for s in range(LAYERS)]
+
+        def turn_w(s, half):
+            turn(sorted_words(w_raw[s][half], 0), identity, w_turned[s][:, half * 2 * WIDTH : (half + 1) * 2 * WIDTH])
+
+        def quantize_w(s):
+            w_mx.append(quantize(keep, "w%d" % s, w_turned[s][:], E4M3))
+
+        turn_w(0, 0)
+        turn_w(0, 1)
+        latest = turn_g(sorted_words(g_raw[0][0], 0))
+        for s in range(1, LAYERS):
+            turn_w(s, 0)
+            quantize_w(s - 1)
+            turn_w(s, 1)
+            operands = sorted_words(g_raw[s][0], 0)
+            quantize_g(latest)
+            multiply_dx(s - 1)
+            latest = turn_g(operands)
+        second = [turn_g(sorted_words(g_raw[0][0], 1))]
+        quantize_w(LAYERS - 1)
+        second.append(turn_g(sorted_words(g_raw[1][0], 1)))
+        operands = sorted_words(g_raw[2][0], 1)
+        quantize_g(latest)
+        multiply_dx(LAYERS - 1)
+        second.append(turn_g(operands))
+        quantize_g(second[0])
+        multiply_dx(LAYERS)
+        quantize_g(second[1])
+        multiplied = LAYERS + 1
+        unquantized = second[2:]
+
+        steps = ["g"] + (PASSES - DIRECT) * ["g", "g", "there", "g", "back"] + ["g", "g"]
+        vector_tiles = [(0, 0), (X, 3), (1, 0), (0, 1), (1, 1), (X, 2), (0, 2), (1, 2), (0, 3), (1, 3)]
+        early_key, late_key = (2, 2), (X, 1)
+        early_tile = keep.tile([P, PACK * WIDTH], BF16, name="early_tile", align_bytes=64)
+        late_tile = keep.tile([P, PACK * WIDTH], BF16, name="late_tile", align_bytes=64)
+        next_bank, next_tile, next_quarter = 2 * LAYERS, 0, 0
+        x_window = []
+        for n, step in enumerate(steps):
+            turned = []
+            if step == "g":
+                for bank in (next_bank, next_bank + 1):
+                    place, s = divmod(bank, LAYERS)
+                    turned.append(turn_g(every_second_word(g_raw[s][place // 2], place % 2)))
+                next_bank = next_bank + 2
+            elif step == "there":
+                x_there = transpose_words(x_tokens[:].bitcast(F32), to_window, "x_there")
             else:
-                nc.sync.dma_start(out=dx_quads[first : first + P // 2, slots, :], in_=result[0 : P // 2])
-                nc.sync.dma_start(out=dx_quads[0 : P // 2, slots, :], in_=result[P // 2 : P])
+                x_window.append(transpose_words(x_there[:], identity, "x_back"))
 
-        X = LAYERS
-        token_work = [
-            [(0, 0), (1, 0)], [(2, 0)], [(0, 1), (1, 1)], [(2, 1)],
-            [(0, 2), (1, 2)], [(X, 0)], [(X, 1), (X, 2)], [(0, 3)],
-        ]
-        late_work = [(X, 3), (1, 3), (2, 2), (2, 3)]
+            key = None
+            if step != "there" and next_tile < len(vector_tiles):
+                key = vector_tiles[next_tile]
+                tokens = interleave_on_vector(key)
+                next_tile = next_tile + 1
+            for grouped in unquantized[:1]:
+                quantize_g(grouped)
+            if key and key[0] == X:
+                x_tokens = tokens
+            elif key and next_tile < len(vector_tiles):
+                quantize_tokens(key, tokens[:])
+            for grouped in unquantized[1:]:
+                quantize_g(grouped)
+            if step == "there" and x_window:
+                quantize_tokens((X, 3), x_window[0][:].bitcast(BF16))
+            unquantized = turned
 
-        turned = []
-        accs = new_accs()
-        for s in range(LAYERS):
-            turn_weight(s)
-            grouped = turn_grad(s, 0)
-            if s < 2:
-                key = token_work[0][s]
-                tokens = interleave(key)
-            turned.append(quantize_grad(grouped))
-            if s < 2:
-                quantize_tokens(key, tokens)
-            if s > 0:
-                for j in range(2):
-                    dx_pass(accs, turned, s - 1, j)
-
-        for half in range(1, HALVES + 1):
-            before = turned
-            if half < HALVES:
-                keys = token_work[half]
-                turned = []
-                tokens = interleave(keys[0])
-                turned.append(quantize_grad(turn_grad(0, half)))
-                quantize_tokens(keys[0], tokens)
-                turned.append(quantize_grad(turn_grad(1, half)))
-                if len(keys) > 1:
-                    tokens = interleave(keys[1])
-                turned.append(quantize_grad(turn_grad(2, half)))
-                if len(keys) > 1:
-                    quantize_tokens(keys[1], tokens)
-            if half == 1:
-                for j in range(2):
-                    dx_pass(accs, before, LAYERS - 1, j)
+            if n == len(steps) - 1:
+                for quarter in range(4):
+                    interleave_on_scalar(late_key, late_tile, quarter)
+                for grouped in unquantized:
+                    quantize_g(grouped)
+                count = len(g_mx) - multiplied
             else:
-                accs = new_accs()
-                for j in range(2):
-                    for s in range(LAYERS):
-                        dx_pass(accs, before, s, j)
-            store_dx(accs, half - 1)
+                count = max(1, len(g_mx) - multiplied - HELD_BACK)
+            for bank in range(multiplied, multiplied + count):
+                multiply_dx(bank)
+            multiplied = multiplied + count
+            if step == "g" and "there" in steps[:n] and next_quarter < 4:
+                interleave_on_scalar(early_key, early_tile, next_quarter)
+                next_quarter = next_quarter + 1
 
-        tokens = [interleave(late_work[0])]
-        for i in range(len(late_work)):
-            if i + 1 < len(late_work):
-                tokens.append(interleave(late_work[i + 1]))
-            quantize_tokens(late_work[i], tokens[i])
+        x_first = interleave_on_vector((X, 0))
+        quantize_tokens((X, 2), x_window[1][:].bitcast(BF16))
+        quantize_tokens((X, 0), x_first[:])
+        quantize_tokens(late_key, late_tile[:])
+        quantize_tokens(vector_tiles[-1], tokens[:])
+        last_tiles = [interleave_on_vector((2, 0)), interleave_on_vector((2, 1))]
+        quantize_tokens((2, 0), last_tiles[0][:])
+        last_tiles.append(interleave_on_vector((2, 3)))
+        quantize_tokens((2, 1), last_tiles[1][:])
+        quantize_tokens(early_key, early_tile[:])
+        quantize_tokens((2, 3), last_tiles[2][:])
 
-        for s in range(LAYERS):
-            for t in range(C_TILES):
-                acc = psum_sum.tile([P, F], F32, name="acc")
+        def multiply_dw(acc, s, m_tile, r, start, stop):
+            multiply(acc, token_mx[(X, r)], m_tile, E4M3, token_mx[(s, r)], E5M2, start, stop)
+
+        def store_dw(acc, s, m_tile):
+            result = results.tile([P, WIDTH], F32, name="result")
+            nc.scalar.copy(out=result[:], in_=acc[:])
+            nc.sync.dma_start(out=dws[s][m_tile], in_=result[:])
+
+        m_tiles = range(WIDTH // P)
+        open_sums = [psum_turn.tile([P, WIDTH], F32, name="bank") for m_tile in m_tiles]
+        pass_order = (3, 2, 0, 1)
+        for r in pass_order:
+            for m_tile in m_tiles:
+                multiply_dw(open_sums[m_tile], 0, m_tile, r, r == pass_order[0], r == pass_order[-1])
+        for m_tile in m_tiles:
+            store_dw(open_sums[m_tile], 0, m_tile)
+        for s in range(1, LAYERS):
+            for m_tile in m_tiles:
+                acc = psum_sum.tile([P, WIDTH], F32, name="acc")
                 for r in range(PASSES):
-                    mx(acc, token_mx[(X, r)], slice(t * P, (t + 1) * P), E4M3, token_mx[(s, r)], E5M2,
-                       r == 0, r == PASSES - 1)
-                result = results.tile([P, F], F32, name="dw_result", bufs=4)
-                nc.scalar.copy(out=result[:], in_=acc[:])
-                nc.sync.dma_start(out=dws[s][t], in_=result[:])
+                    multiply_dw(acc, s, m_tile, r, r == 0, r == PASSES - 1)
+                store_dw(acc, s, m_tile)

from contextlib import ExitStack

import concourse.mybir as mybir
from concourse.masks import make_identity

F32 = mybir.dt.float32
BF16 = mybir.dt.bfloat16
U32 = mybir.dt.uint32
U8 = mybir.dt.uint8
E4M3 = mybir.dt.float8_e4m3fn_x4
E5M2 = mybir.dt.float8_e5m2_x4

P = 128
PACK = 4
WIDTH = 512
LAYERS = 3
PASSES = 4
WIN = 8
SHIFT = 4
ROWS = 32
QUADS = 16
X = LAYERS
DIRECT = 2
HELD_BACK = 2

FLOPS = 2 * 2 * 2048 * 512 * 1536
BYTES = 2 * (2048 * 512 + 3 * 512 * 512 + 3 * 2048 * 512) + 4 * (2048 * 512 + 3 * 512 * 512)


def tile_windowattentionblock_pa_v_kernel(
    tc, x, wq, bq, wk, bk, wv, bv, grad_0, grad_1, grad_2, out_0, out_1, out_2, out_3
):
    nc = tc.nc
    weights = [w.rearrange("(j p) h d -> p j (h d)", p=P) for w in (wq, wk, wv)]
    grads = [
        g.rearrange("n t h d -> (n t) (h d)").rearrange("(r p j) f -> r p (j f)", p=P, j=PACK)
        for g in (grad_0, grad_1, grad_2)
    ]
    x_quads = x.rearrange("b row (q j) c -> (b row) q (j c)", j=PACK)
    x_image = x_quads.rearrange("row q e -> (row q) e")
    dx_image = out_0.rearrange("b row (q j) c -> (b row q) j c", j=PACK)
    dws = [o.rearrange("(m p) h d -> m p (h d)", p=P) for o in (out_1, out_2, out_3)]

    with ExitStack() as ctx:
        keep = ctx.enter_context(tc.tile_pool(name="keep", bufs=1))
        stage = ctx.enter_context(tc.tile_pool(name="stage", bufs=4))
        results = ctx.enter_context(tc.tile_pool(name="results", bufs=8))
        psum_turn = ctx.enter_context(tc.psum_pool(name="psum_turn", bufs=4))
        psum_sum = ctx.enter_context(tc.psum_pool(name="psum_sum", bufs=4))
        ctx.enter_context(tc.manual_schedule())

        w_raw = [[keep.tile([P, 2 * WIDTH], BF16, name="w_raw%d_%d" % (s, a)) for a in range(2)] for s in range(LAYERS)]
        g_raw = [
            [keep.tile([P, PACK * WIDTH], BF16, name="g_raw%d_%d" % (s, r)) for r in range(PASSES)]
            for s in range(LAYERS)
        ]
        x_direct = keep.tile([P, DIRECT, PACK * WIDTH], BF16, name="x_direct")
        x_raw = {r: keep.tile([P, PACK * WIDTH], BF16, name="x_raw%d" % r) for r in range(DIRECT, PASSES)}

        def image_ranges(r):
            first = (r * WIN + SHIFT) * QUADS
            if r < PASSES - 1:
                return [(slice(0, P), slice(first, first + P))]
            return [(slice(0, P // 2), slice(first, first + P // 2)), (slice(P // 2, P), slice(0, P // 2))]

        def load_g(r, cols):
            for s in range(LAYERS):
                nc.sync.dma_start(out=g_raw[s][r][:, cols], in_=grads[s][r][:, cols])

        def load_x_image(r):
            for parts, quads in image_ranges(r):
                nc.sync.dma_start(out=x_raw[r][parts, :], in_=x_image[quads, :])

        first_half, second_half = slice(0, 2 * WIDTH), slice(2 * WIDTH, PACK * WIDTH)
        for s in range(LAYERS):
            for half in range(2):
                nc.sync.dma_start(
                    out=w_raw[s][half][:].rearrange("p (j f) -> p j f", j=2),
                    in_=weights[s][:, 2 * half : 2 * half + 2, :],
                )
            nc.sync.dma_start(out=g_raw[s][0][:, first_half], in_=grads[s][0][:, first_half])
        load_g(0, second_half)
        for r in range(1, PASSES):
            load_g(r, slice(0, PACK * WIDTH))
            if r <= PASSES - DIRECT:
                load_x_image(PASSES - r)
        for h in range(2):
            for n in range(WIN):
                gj = n // 2 + (n % 2) * (WIN // 2)
                rows = x_quads[SHIFT : SHIFT + DIRECT * WIN, (2 * gj + h + 1) % QUADS, :]
                nc.sync.dma_start(
                    out=x_direct[2 * WIN * gj + h : 2 * WIN * (gj + 1) : 2, :, :],
                    in_=rows.rearrange("(r ti) e -> ti r e", ti=WIN),
                )

        def quad_copies(window_cols, image_cols):
            win = window_cols.rearrange("p (gj ti h) -> p ti gj h", ti=WIN, h=2)
            img = image_cols.rearrange("p (ti a e) -> p ti a e", ti=WIN, e=2)
            return [
                (win[:, :, :, 0], img[:, :, :, 1]),
                (win[:, :, 0 : WIN - 1, 1], img[:, :, 1:WIN, 0]),
                (win[:, :, WIN - 1 : WIN, 1], img[:, :, 0:1, 0]),
            ]

        identity = keep.tile([P, P], F32, name="identity")
        to_image = keep.tile([P, P], F32, name="to_image")
        to_window = keep.tile([P, P], F32, name="to_window")
        make_identity(nc, identity[:])
        for win, img in quad_copies(identity[:], to_image[:]):
            nc.vector.tensor_copy(out=img, in_=win)
        for win, img in quad_copies(to_window[:], identity[:]):
            nc.vector.tensor_copy(out=win, in_=img)

        def quantize(pool, name, grouped, fmt, bufs=None):
            cols = grouped.shape[1] // PACK
            codes = pool.tile([P, cols], U32, name=name + "_codes", align_bytes=64, bufs=bufs)
            scales = pool.tile([P, cols], U8, name=name + "_scales", align_bytes=64, bufs=bufs)
            nc.vector.quantize_mx(out=codes[:].bitcast(fmt), scales=scales[:], in_=grouped)
            return codes, scales

        def multiply(acc, stationary, m_tile, stationary_fmt, moving, moving_fmt, start, stop):
            cols = slice(m_tile * P, (m_tile + 1) * P)
            nc.tensor.matmul_mx(
                out=acc[:],
                lhsT=stationary[0][:, cols].bitcast(stationary_fmt),
                lhsT_scale=stationary[1][:, cols],
                rhs=moving[0][:].bitcast(moving_fmt),
                rhs_scale=moving[1][:],
                start=start,
                stop=stop,
            )

        def every_second_word(raw, half):
            words = raw[:].bitcast(F32)
            starts = [(2 * half + j) * 2 * P for j in range(2)]
            return [words[:, start + u : start + 2 * P : 2] for start in starts for u in range(2)]

        def sorted_words(raw, half):
            ordered = stage.tile([P, WIDTH], F32, name="ordered")
            nc.vector.tensor_copy(
                out=ordered[:].rearrange("p (j u q) -> p j u q", j=2, u=2),
                in_=raw[:].bitcast(F32)[:, half * WIDTH : (half + 1) * WIDTH].rearrange(
                    "p (j q u) -> p j u q", j=2, u=2
                ),
            )
            return [ordered[:, i * P : (i + 1) * P] for i in range(4)]

        def transpose_bank(operands, moving):
            bank = psum_turn.tile([P, WIDTH], F32, name="bank")
            for i, operand in enumerate(operands):
                nc.tensor.transpose(bank[:, i * P : (i + 1) * P], operand, moving[:])
            return bank

        def turn(operands, moving, grouped):
            bank = transpose_bank(operands, moving)
            nc.scalar.copy(
                out=grouped.bitcast(F32).rearrange("p (j col u) -> p j col u", j=2, u=2),
                in_=bank[:].rearrange("p (j u col) -> p j col u", j=2, u=2),
            )

        def turn_g(operands):
            grouped = stage.tile([P, 2 * WIDTH], BF16, name="g_turned", align_bytes=64, bufs=5)
            turn(operands, to_image, grouped[:])
            return grouped

        def transpose_words(words, moving, name):
            moved = stage.tile([P, 2 * WIDTH], F32, name=name, align_bytes=64, bufs=1)
            for half in range(2):
                blocks = [words[:, (4 * half + i) * P : (4 * half + i + 1) * P] for i in range(4)]
                bank = transpose_bank(blocks, moving)
                nc.scalar.copy(out=moved[:, half * WIDTH : (half + 1) * WIDTH], in_=bank[:])
            return moved

        def interleave(copy, key, grouped, cols):
            s, r = key
            if s < LAYERS:
                raw = g_raw[s][r][:]
            else:
                raw = x_direct[:, r, :] if r < DIRECT else x_raw[r][:]
            copy(
                out=grouped[:, PACK * cols.start : PACK * cols.stop].rearrange("p (c i t) -> p c t i", i=4, t=PACK),
                in_=raw.rearrange("p (t c) -> p t c", t=PACK)[:, :, cols].rearrange("p t (c i) -> p c t i", i=4),
            )

        def interleave_on_vector(key):
            grouped = stage.tile([P, PACK * WIDTH], BF16, name="tokens", align_bytes=64, bufs=3)
            interleave(nc.vector.tensor_copy, key, grouped, slice(0, WIDTH))
            return grouped

        def interleave_on_scalar(key, grouped, quarter):
            interleave(nc.scalar.copy, key, grouped, slice(quarter * P, (quarter + 1) * P))

        w_mx = []
        g_mx = []
        token_mx = {}
        dx_sums = []

        def quantize_g(grouped):
            g_mx.append(quantize(stage, "g", grouped[:], E5M2, bufs=8))

        def quantize_tokens(key, grouped):
            token_mx[key] = quantize(keep, "tokens%d_%d" % key, grouped, E4M3 if key[0] == X else E5M2)

        def multiply_dx(bank):
            place, s = divmod(bank, LAYERS)
            if s == 0:
                dx_sums.append([psum_sum.tile([P, WIDTH], F32, name="acc") for j in range(2)])
            for j in range(2):
                multiply(dx_sums[place][j], g_mx[bank], j, E5M2, w_mx[s], E4M3, s == 0, s == LAYERS - 1)
            if s == LAYERS - 1:
                r, half = divmod(place, 2)
                result = results.tile([P, 2, WIDTH], F32, name="result")
                for j in range(2):
                    nc.scalar.copy(out=result[:, j, :], in_=dx_sums[place][j][:])
                for parts, quads in image_ranges(r):
                    nc.sync.dma_start(out=dx_image[quads, 2 * half : 2 * half + 2, :], in_=result[parts])

        w_turned = [keep.tile([P, PACK * WIDTH], BF16, name="w_turned%d" % s, align_bytes=64) for s in range(LAYERS)]

        def turn_w(s, half):
            turn(sorted_words(w_raw[s][half], 0), identity, w_turned[s][:, half * 2 * WIDTH : (half + 1) * 2 * WIDTH])

        def quantize_w(s):
            w_mx.append(quantize(keep, "w%d" % s, w_turned[s][:], E4M3))

        turn_w(0, 0)
        turn_w(0, 1)
        latest = turn_g(sorted_words(g_raw[0][0], 0))
        for s in range(1, LAYERS):
            turn_w(s, 0)
            quantize_w(s - 1)
            turn_w(s, 1)
            operands = sorted_words(g_raw[s][0], 0)
            quantize_g(latest)
            multiply_dx(s - 1)
            latest = turn_g(operands)
        second = [turn_g(sorted_words(g_raw[0][0], 1))]
        quantize_w(LAYERS - 1)
        second.append(turn_g(sorted_words(g_raw[1][0], 1)))
        operands = sorted_words(g_raw[2][0], 1)
        quantize_g(latest)
        multiply_dx(LAYERS - 1)
        second.append(turn_g(operands))
        quantize_g(second[0])
        multiply_dx(LAYERS)
        quantize_g(second[1])
        multiplied = LAYERS + 1
        unquantized = second[2:]

        steps = ["g"] + (PASSES - DIRECT) * ["g", "g", "there", "g", "back"] + ["g", "g"]
        vector_tiles = [(0, 0), (X, 3), (1, 0), (0, 1), (1, 1), (X, 2), (0, 2), (1, 2), (0, 3), (1, 3)]
        early_key, late_key = (2, 2), (X, 1)
        early_tile = keep.tile([P, PACK * WIDTH], BF16, name="early_tile", align_bytes=64)
        late_tile = keep.tile([P, PACK * WIDTH], BF16, name="late_tile", align_bytes=64)
        next_bank, next_tile, next_quarter = 2 * LAYERS, 0, 0
        x_window = []
        for n, step in enumerate(steps):
            turned = []
            if step == "g":
                for bank in (next_bank, next_bank + 1):
                    place, s = divmod(bank, LAYERS)
                    turned.append(turn_g(every_second_word(g_raw[s][place // 2], place % 2)))
                next_bank = next_bank + 2
            elif step == "there":
                x_there = transpose_words(x_tokens[:].bitcast(F32), to_window, "x_there")
            else:
                x_window.append(transpose_words(x_there[:], identity, "x_back"))

            key = None
            if step != "there" and next_tile < len(vector_tiles):
                key = vector_tiles[next_tile]
                tokens = interleave_on_vector(key)
                next_tile = next_tile + 1
            for grouped in unquantized[:1]:
                quantize_g(grouped)
            if key and key[0] == X:
                x_tokens = tokens
            elif key and next_tile < len(vector_tiles):
                quantize_tokens(key, tokens[:])
            for grouped in unquantized[1:]:
                quantize_g(grouped)
            if step == "there" and x_window:
                quantize_tokens((X, 3), x_window[0][:].bitcast(BF16))
            unquantized = turned

            if n == len(steps) - 1:
                for quarter in range(4):
                    interleave_on_scalar(late_key, late_tile, quarter)
                for grouped in unquantized:
                    quantize_g(grouped)
                count = len(g_mx) - multiplied
            else:
                count = max(1, len(g_mx) - multiplied - HELD_BACK)
            for bank in range(multiplied, multiplied + count):
                multiply_dx(bank)
            multiplied = multiplied + count
            if step == "g" and "there" in steps[:n] and next_quarter < 4:
                interleave_on_scalar(early_key, early_tile, next_quarter)
                next_quarter = next_quarter + 1

        x_first = interleave_on_vector((X, 0))
        quantize_tokens((X, 2), x_window[1][:].bitcast(BF16))
        quantize_tokens((X, 0), x_first[:])
        quantize_tokens(late_key, late_tile[:])
        quantize_tokens(vector_tiles[-1], tokens[:])
        last_tiles = [interleave_on_vector((2, 0)), interleave_on_vector((2, 1))]
        quantize_tokens((2, 0), last_tiles[0][:])
        last_tiles.append(interleave_on_vector((2, 3)))
        quantize_tokens((2, 1), last_tiles[1][:])
        quantize_tokens(early_key, early_tile[:])
        quantize_tokens((2, 3), last_tiles[2][:])

        def multiply_dw(acc, s, m_tile, r, start, stop):
            multiply(acc, token_mx[(X, r)], m_tile, E4M3, token_mx[(s, r)], E5M2, start, stop)

        def store_dw(acc, s, m_tile):
            result = results.tile([P, WIDTH], F32, name="result")
            nc.scalar.copy(out=result[:], in_=acc[:])
            nc.sync.dma_start(out=dws[s][m_tile], in_=result[:])

        m_tiles = range(WIDTH // P)
        open_sums = [psum_turn.tile([P, WIDTH], F32, name="bank") for m_tile in m_tiles]
        pass_order = (3, 2, 0, 1)
        for r in pass_order:
            for m_tile in m_tiles:
                multiply_dw(open_sums[m_tile], 0, m_tile, r, r == pass_order[0], r == pass_order[-1])
        for m_tile in m_tiles:
            store_dw(open_sums[m_tile], 0, m_tile)
        for s in range(1, LAYERS):
            for m_tile in m_tiles:
                acc = psum_sum.tile([P, WIDTH], F32, name="acc")
                for r in range(PASSES):
                    multiply_dw(acc, s, m_tile, r, r == 0, r == PASSES - 1)
                store_dw(acc, s, m_tile)
